import numpy as np
import ml_dtypes


def mxq(x, axis, fmt="e4m3"):
    dtype, down = {"e4m3": (ml_dtypes.float8_e4m3fn, 7), "e5m2": (ml_dtypes.float8_e5m2, 14)}[fmt]
    v = np.moveaxis(np.asarray(x, np.float32).astype(ml_dtypes.bfloat16).astype(np.float64), axis, -1)
    blocks = v.reshape(v.shape[:-1] + (-1, 32))
    amax = np.abs(blocks).max(-1, keepdims=True)
    byte = np.maximum(np.where(amax > 0, np.frexp(amax)[1] - 1 + 127, 0) - down, 1)
    scale = np.exp2(byte - 127.0)
    codes = (blocks / scale).astype(np.float32).astype(dtype).astype(np.float64)
    return np.moveaxis((codes * scale).reshape(v.shape), -1, axis)


WIDE = False


def mx_kscale(k):
    if not WIDE:
        return np.ones(k)
    levels = np.array([10, -10, 5, -5, 0])
    a = np.random.permutation(np.resize(levels, k // 512 * 4)).reshape(k // 512, 4)
    idx = np.arange(k)
    return np.exp2(a[idx // 512, idx % 128 // 32])


BF16 = ml_dtypes.bfloat16


def bf(x):
    return np.asarray(x, np.float32).astype(BF16)


def f64(x):
    return np.asarray(x).astype(np.float64)


B, N, K, H, C_E, M = 2, 256, 32, 256, 1024, 512
SCALE = 30.0


def setup_inputs():
    s = mx_kscale(M)
    return {"h2": bf(np.random.standard_normal((B, N, K, M)) * 0.65 * s),
            "h_V": bf(np.random.standard_normal((B, N, H))),
            "mask_attend": bf(np.random.uniform(size=(B, N, K)) < 0.9),
            "W3_w": bf(np.random.standard_normal((M, H)) * 4.0 / np.sqrt(M) / s[:, None]),
            "W3_b": bf(np.random.standard_normal(H) * 0.1)}


def reference(h2, h_V, mask_attend, W3_w, W3_b):
    h_message = (mxq(f64(h2), 3, "e4m3") @ mxq(f64(W3_w), 0, "e4m3")) + f64(W3_b)
    h_message = f64(mask_attend)[..., None] * h_message
    dh = np.sum(h_message, axis=-2) / SCALE
    return f64(h_V) + dh

@@ -1,0 +1,203 @@
+from contextlib import ExitStack
+
+import concourse.masks as masks
+import concourse.mybir as mybir
+
+F32 = mybir.dt.float32
+BF16 = mybir.dt.bfloat16
+U32 = mybir.dt.uint32
+U8 = mybir.dt.uint8
+FP8X4 = mybir.dt.float8_e4m3fn_x4
+MULT = mybir.AluOpType.mult
+ADD = mybir.AluOpType.add
+
+P = 128
+PACK = 4
+NODES = 2 * 256
+EDGES = 32
+M = 512
+H = 256
+SCALE = 30.0
+
+NODE_TILES = NODES // P
+WORDS = M // 2
+HALVES = WORDS // P
+GROUP = 4
+GROUPS_PER_TILE = EDGES // GROUP
+N_GROUPS = NODE_TILES * GROUPS_PER_TILE
+BANK_EDGES = 2
+GROUPS_PER_RUN = 2
+N_RUNS = N_GROUPS // GROUPS_PER_RUN
+
+FLOPS = 2 * NODES * EDGES * M * H
+
+
+def tile_declayerj_pb_t_kernel(tc, h2, h_V, mask_attend, W3_w, W3_b, out):
+    nc = tc.nc
+    h2_rows = h2.rearrange("b n k m -> (b n) (k m)")
+    out_rows = out.rearrange("b n h -> (b n) h")
+
+    with ExitStack() as ctx:
+        const = ctx.enter_context(tc.tile_pool(name="const", bufs=1))
+        x_pool = ctx.enter_context(tc.tile_pool(name="x", bufs=N_GROUPS))
+        sel_pool = ctx.enter_context(tc.tile_pool(name="sel", bufs=4 * GROUPS_PER_RUN))
+        stage = ctx.enter_context(tc.tile_pool(name="stage", bufs=3 * GROUPS_PER_RUN))
+        tail = ctx.enter_context(tc.tile_pool(name="tail", bufs=2))
+        xt_pool = ctx.enter_context(tc.psum_pool(name="xt", bufs=6))
+        acc_pool = ctx.enter_context(tc.psum_pool(name="acc", bufs=2))
+        ctx.enter_context(tc.manual_schedule())
+
+        ident = const.tile([P, P], F32)
+        masks.make_identity(nc, ident[:])
+        ones = const.tile([P, P], BF16)
+        nc.vector.memset(ones[:], 1.0)
+        bias_rows = const.tile([P, H], BF16)
+        nc.vector.memset(bias_rows[:], 0.0)
+
+        mask_bf = const.tile([P, NODE_TILES, EDGES], BF16)
+        nc.sync.dma_start(
+            out=mask_bf[:],
+            in_=mask_attend.rearrange("b n k -> (b n) k").rearrange("(i p) k -> p i k", p=P),
+        )
+        nc.sync.dma_start(out=bias_rows[0:1, :], in_=W3_b.unsqueeze(0))
+        w_raw = const.tile([P, PACK, H], BF16)
+        hv = const.tile([P, NODE_TILES, H], BF16)
+        x_of = {}
+        for g in range(N_GROUPS):
+            i, q = divmod(g, GROUPS_PER_TILE)
+            x_of[g] = x_pool.tile([P, GROUP * M], BF16, name="x")
+            nc.sync.dma_start(
+                out=x_of[g][:],
+                in_=h2_rows[i * P : (i + 1) * P, q * GROUP * M : (q + 1) * GROUP * M],
+            )
+            if g == 0:
+                nc.sync.dma_start(
+                    out=w_raw[:].rearrange("p (u e) h -> p u (e h)", u=HALVES),
+                    in_=W3_w.rearrange("(u p e) h -> p u (e h)", u=HALVES, p=P),
+                )
+            if g == GROUPS_PER_RUN:
+                nc.sync.dma_start(
+                    out=hv[:],
+                    in_=h_V.rearrange("b n h -> (b n) h").rearrange("(i p) h -> p i h", p=P),
+                )
+
+        bias_ps = acc_pool.tile([P, H], F32, name="bias_ps", tag="acc")
+        nc.tensor.matmul(out=bias_ps[:], lhsT=ones[:], rhs=bias_rows[:], start=True, stop=True)
+        bias_all = const.tile([P, H], F32)
+        nc.scalar.copy(out=bias_all[:], in_=bias_ps[:])
+
+        mask_f32 = const.tile([P, NODE_TILES, EDGES], F32)
+        nc.vector.tensor_copy(out=mask_f32[:], in_=mask_bf[:])
+        count = const.tile([P, NODE_TILES], F32)
+        nc.vector.reduce_sum(out=count[:], in_=mask_f32[:], axis=mybir.AxisListType.X)
+        count_scaled = const.tile([P, NODE_TILES], F32)
+        nc.vector.tensor_scalar_mul(out=count_scaled[:], in0=count[:], scalar1=1.0 / SCALE)
+
+        sel_of = {}
+        grouped_of = {}
+        codes_of = {}
+        scales_of = {}
+        acc_of = {}
+
+        def build_selectors(g):
+            i, q = divmod(g, GROUPS_PER_TILE)
+            sel_of[g] = sel_pool.tile([P, GROUP, P], F32, name="sel")
+            for j in range(GROUP):
+                k = q * GROUP + j
+                nc.vector.tensor_scalar_mul(
+                    out=sel_of[g][:, j, :], in0=ident[:], scalar1=mask_f32[:, i, k : k + 1]
+                )
+
+        def transpose_group(g):
+            x_words = x_of[g][:].bitcast(F32)
+            grouped_of[g] = stage.tile([P, GROUP * P * PACK], BF16, name="grouped", align_bytes=64)
+            grouped_words = grouped_of[g][:].bitcast(F32)
+            bank_words = BANK_EDGES * P * HALVES
+            for b in range(GROUP // BANK_EDGES):
+                xt = xt_pool.tile([P, BANK_EDGES, HALVES, P], F32, name="xt")
+                for jj in range(BANK_EDGES):
+                    j = b * BANK_EDGES + jj
+                    for u in range(HALVES):
+                        first = j * WORDS + u * P
+                        nc.tensor.transpose(
+                            xt[:, jj, u, :], x_words[:, first : first + P], sel_of[g][:, j, :]
+                        )
+                nc.scalar.copy(
+                    out=grouped_words[:, b * bank_words : (b + 1) * bank_words].rearrange(
+                        "p (j n u) -> p j n u", j=BANK_EDGES, u=HALVES
+                    ),
+                    in_=xt[:].rearrange("p j u n -> p j n u"),
+                )
+
+        def quantise_group(g):
+            codes_of[g] = stage.tile([P, GROUP * P], U32, name="codes", align_bytes=64)
+            scales_of[g] = stage.tile([P, GROUP * P], U8, name="scales", align_bytes=64)
+            nc.vector.quantize_mx(
+                out=codes_of[g][:].bitcast(FP8X4), scales=scales_of[g][:], in_=grouped_of[g][:]
+            )
+
+        def multiply_group(g):
+            i, q = divmod(g, GROUPS_PER_TILE)
+            if q == 0:
+                acc_of[i] = acc_pool.tile([P, H], F32, name="acc", tag="acc")
+            for j in range(GROUP):
+                k = q * GROUP + j
+                nodes = slice(j * P, (j + 1) * P)
+                nc.tensor.matmul_mx(
+                    out=acc_of[i][:],
+                    lhsT=codes_of[g][:, nodes].bitcast(FP8X4),
+                    lhsT_scale=scales_of[g][:, nodes],
+                    rhs=w_codes[:].bitcast(FP8X4),
+                    rhs_scale=w_scales[:],
+                    start=(k == 0),
+                    stop=(k == EDGES - 1),
+                )
+            if q == GROUPS_PER_TILE - 1:
+                finish_node_tile(i)
+
+        def finish_node_tile(i):
+            rest = tail.tile([P, H], F32, name="rest")
+            nc.vector.scalar_tensor_tensor(
+                out=rest[:],
+                in0=bias_all[:],
+                scalar=count_scaled[:, i : i + 1],
+                in1=hv[:, i, :],
+                op0=MULT,
+                op1=ADD,
+            )
+            result = tail.tile([P, H], F32, name="result")
+            nc.vector.scalar_tensor_tensor(
+                out=result[:], in0=acc_of[i][:], scalar=1.0 / SCALE, in1=rest[:], op0=MULT, op1=ADD
+            )
+            nc.sync.dma_start(out=out_rows[i * P : (i + 1) * P, :], in_=result[:])
+
+        def groups_of_run(r):
+            return range(r * GROUPS_PER_RUN, (r + 1) * GROUPS_PER_RUN)
+
+        for g in groups_of_run(0):
+            build_selectors(g)
+        w_grouped = const.tile([P, H, PACK], BF16, align_bytes=64)
+        nc.vector.tensor_copy(out=w_grouped[:], in_=w_raw[:].rearrange("p t h -> p h t"))
+        for g in groups_of_run(1):
+            build_selectors(g)
+        w_codes = const.tile([P, H], U32, align_bytes=64)
+        w_scales = const.tile([P, H], U8, align_bytes=64)
+        nc.vector.quantize_mx(
+            out=w_codes[:].bitcast(FP8X4),
+            scales=w_scales[:],
+            in_=w_grouped[:].rearrange("p h t -> p (h t)"),
+        )
+
+        for r in range(N_RUNS + 1):
+            if r < N_RUNS:
+                for g in groups_of_run(r):
+                    transpose_group(g)
+            if r + 2 < N_RUNS:
+                for g in groups_of_run(r + 2):
+                    build_selectors(g)
+            if r < N_RUNS:
+                for g in groups_of_run(r):
+                    quantise_group(g)
+            if r >= 1:
+                for g in groups_of_run(r - 1):
+                    multiply_group(g)

@@ -26,22 +26,26 @@ GROUP = 4
 GROUPS_PER_TILE = EDGES // GROUP
 N_GROUPS = NODE_TILES * GROUPS_PER_TILE
 BANK_EDGES = 2
-GROUPS_PER_RUN = 2
+GROUPS_PER_RUN = 4
 N_RUNS = N_GROUPS // GROUPS_PER_RUN
+LAG = 2
 
 FLOPS = 2 * NODES * EDGES * M * H
 
 
 def tile_declayerj_pb_t_kernel(tc, h2, h_V, mask_attend, W3_w, W3_b, out):
     nc = tc.nc
-    h2_rows = h2.rearrange("b n k m -> (b n) (k m)")
-    out_rows = out.rearrange("b n h -> (b n) h")
+    h2_nodes = h2.rearrange("b n k m -> (b n) (k m)").rearrange("(p i) f -> p i f", p=P)
+    mask_nodes = mask_attend.rearrange("b n k -> (b n) k").rearrange("(p i) k -> p i k", p=P)
+    hv_nodes = h_V.rearrange("b n h -> (b n) h").rearrange("(p i) h -> p i h", p=P)
+    out_nodes = out.rearrange("b n h -> (b n) h").rearrange("(p i) h -> p i h", p=P)
 
     with ExitStack() as ctx:
         const = ctx.enter_context(tc.tile_pool(name="const", bufs=1))
         x_pool = ctx.enter_context(tc.tile_pool(name="x", bufs=N_GROUPS))
-        sel_pool = ctx.enter_context(tc.tile_pool(name="sel", bufs=4 * GROUPS_PER_RUN))
-        stage = ctx.enter_context(tc.tile_pool(name="stage", bufs=3 * GROUPS_PER_RUN))
+        sel_pool = ctx.enter_context(tc.tile_pool(name="sel", bufs=2 * GROUPS_PER_RUN))
+        grouped_pool = ctx.enter_context(tc.tile_pool(name="grouped", bufs=GROUPS_PER_RUN + LAG))
+        mx_pool = ctx.enter_context(tc.tile_pool(name="mx", bufs=2 * GROUPS_PER_RUN))
         tail = ctx.enter_context(tc.tile_pool(name="tail", bufs=2))
         xt_pool = ctx.enter_context(tc.psum_pool(name="xt", bufs=6))
         acc_pool = ctx.enter_context(tc.psum_pool(name="acc", bufs=2))
@@ -55,10 +59,7 @@ def tile_declayerj_pb_t_kernel(tc, h2, h_V, mask_attend, W3_w, W3_b, out):
         nc.vector.memset(bias_rows[:], 0.0)
 
         mask_bf = const.tile([P, NODE_TILES, EDGES], BF16)
-        nc.sync.dma_start(
-            out=mask_bf[:],
-            in_=mask_attend.rearrange("b n k -> (b n) k").rearrange("(i p) k -> p i k", p=P),
-        )
+        nc.sync.dma_start(out=mask_bf[:], in_=mask_nodes)
         nc.sync.dma_start(out=bias_rows[0:1, :], in_=W3_b.unsqueeze(0))
         w_raw = const.tile([P, PACK, H], BF16)
         hv = const.tile([P, NODE_TILES, H], BF16)
@@ -68,18 +69,15 @@ def tile_declayerj_pb_t_kernel(tc, h2, h_V, mask_attend, W3_w, W3_b, out):
             x_of[g] = x_pool.tile([P, GROUP * M], BF16, name="x")
             nc.sync.dma_start(
                 out=x_of[g][:],
-                in_=h2_rows[i * P : (i + 1) * P, q * GROUP * M : (q + 1) * GROUP * M],
+                in_=h2_nodes[:, i, q * GROUP * M : (q + 1) * GROUP * M],
             )
             if g == 0:
                 nc.sync.dma_start(
                     out=w_raw[:].rearrange("p (u e) h -> p u (e h)", u=HALVES),
                     in_=W3_w.rearrange("(u p e) h -> p u (e h)", u=HALVES, p=P),
                 )
-            if g == GROUPS_PER_RUN:
-                nc.sync.dma_start(
-                    out=hv[:],
-                    in_=h_V.rearrange("b n h -> (b n) h").rearrange("(i p) h -> p i h", p=P),
-                )
+            if g == GROUPS_PER_TILE - 1:
+                nc.sync.dma_start(out=hv[:], in_=hv_nodes)
 
         bias_ps = acc_pool.tile([P, H], F32, name="bias_ps", tag="acc")
         nc.tensor.matmul(out=bias_ps[:], lhsT=ones[:], rhs=bias_rows[:], start=True, stop=True)
@@ -110,7 +108,9 @@ def tile_declayerj_pb_t_kernel(tc, h2, h_V, mask_attend, W3_w, W3_b, out):
 
         def transpose_group(g):
             x_words = x_of[g][:].bitcast(F32)
-            grouped_of[g] = stage.tile([P, GROUP * P * PACK], BF16, name="grouped", align_bytes=64)
+            grouped_of[g] = grouped_pool.tile(
+                [P, GROUP * P * PACK], BF16, name="grouped", align_bytes=64
+            )
             grouped_words = grouped_of[g][:].bitcast(F32)
             bank_words = BANK_EDGES * P * HALVES
             for b in range(GROUP // BANK_EDGES):
@@ -130,8 +130,8 @@ def tile_declayerj_pb_t_kernel(tc, h2, h_V, mask_attend, W3_w, W3_b, out):
                 )
 
         def quantise_group(g):
-            codes_of[g] = stage.tile([P, GROUP * P], U32, name="codes", align_bytes=64)
-            scales_of[g] = stage.tile([P, GROUP * P], U8, name="scales", align_bytes=64)
+            codes_of[g] = mx_pool.tile([P, GROUP * P], U32, name="codes", align_bytes=64)
+            scales_of[g] = mx_pool.tile([P, GROUP * P], U8, name="scales", align_bytes=64)
             nc.vector.quantize_mx(
                 out=codes_of[g][:].bitcast(FP8X4), scales=scales_of[g][:], in_=grouped_of[g][:]
             )
@@ -169,17 +169,15 @@ def tile_declayerj_pb_t_kernel(tc, h2, h_V, mask_attend, W3_w, W3_b, out):
             nc.vector.scalar_tensor_tensor(
                 out=result[:], in0=acc_of[i][:], scalar=1.0 / SCALE, in1=rest[:], op0=MULT, op1=ADD
             )
-            nc.sync.dma_start(out=out_rows[i * P : (i + 1) * P, :], in_=result[:])
+            nc.sync.dma_start(out=out_nodes[:, i, :], in_=result[:])
 
         def groups_of_run(r):
-            return range(r * GROUPS_PER_RUN, (r + 1) * GROUPS_PER_RUN)
+            return range(r * GROUPS_PER_RUN, min((r + 1) * GROUPS_PER_RUN, N_GROUPS))
 
         for g in groups_of_run(0):
             build_selectors(g)
         w_grouped = const.tile([P, H, PACK], BF16, align_bytes=64)
         nc.vector.tensor_copy(out=w_grouped[:], in_=w_raw[:].rearrange("p t h -> p h t"))
-        for g in groups_of_run(1):
-            build_selectors(g)
         w_codes = const.tile([P, H], U32, align_bytes=64)
         w_scales = const.tile([P, H], U8, align_bytes=64)
         nc.vector.quantize_mx(
@@ -189,15 +187,12 @@ def tile_declayerj_pb_t_kernel(tc, h2, h_V, mask_attend, W3_w, W3_b, out):
         )
 
         for r in range(N_RUNS + 1):
-            if r < N_RUNS:
-                for g in groups_of_run(r):
-                    transpose_group(g)
-            if r + 2 < N_RUNS:
-                for g in groups_of_run(r + 2):
-                    build_selectors(g)
-            if r < N_RUNS:
-                for g in groups_of_run(r):
-                    quantise_group(g)
-            if r >= 1:
-                for g in groups_of_run(r - 1):
-                    multiply_group(g)
+            for g in groups_of_run(r):
+                transpose_group(g)
+            for g in groups_of_run(r + 1):
+                build_selectors(g)
+            for g in groups_of_run(r):
+                quantise_group(g)
+            first = max(r * GROUPS_PER_RUN - LAG, 0)
+            for g in range(first, min((r + 1) * GROUPS_PER_RUN - LAG, N_GROUPS)):
+                multiply_group(g)

@@ -26,6 +26,8 @@ GROUP = 4
 GROUPS_PER_TILE = EDGES // GROUP
 N_GROUPS = NODE_TILES * GROUPS_PER_TILE
 BANK_EDGES = 2
+GROUP_BANKS = GROUP // BANK_EDGES
+BANK_WORDS = BANK_EDGES * WORDS
 GROUPS_PER_RUN = 4
 N_RUNS = N_GROUPS // GROUPS_PER_RUN
 LAG = 2
@@ -92,6 +94,7 @@ def tile_declayerj_pb_t_kernel(tc, h2, h_V, mask_attend, W3_w, W3_b, out):
         nc.vector.tensor_scalar_mul(out=count_scaled[:], in0=count[:], scalar1=1.0 / SCALE)
 
         sel_of = {}
+        xt_of = {}
         grouped_of = {}
         codes_of = {}
         scales_of = {}
@@ -108,26 +111,26 @@ def tile_declayerj_pb_t_kernel(tc, h2, h_V, mask_attend, W3_w, W3_b, out):
 
         def transpose_group(g):
             x_words = x_of[g][:].bitcast(F32)
-            grouped_of[g] = grouped_pool.tile(
-                [P, GROUP * P * PACK], BF16, name="grouped", align_bytes=64
-            )
-            grouped_words = grouped_of[g][:].bitcast(F32)
-            bank_words = BANK_EDGES * P * HALVES
-            for b in range(GROUP // BANK_EDGES):
-                xt = xt_pool.tile([P, BANK_EDGES, HALVES, P], F32, name="xt")
+            for b in range(GROUP_BANKS):
+                xt_of[g, b] = xt_pool.tile([P, BANK_EDGES, HALVES, P], F32, name="xt")
                 for jj in range(BANK_EDGES):
                     j = b * BANK_EDGES + jj
                     for u in range(HALVES):
                         first = j * WORDS + u * P
                         nc.tensor.transpose(
-                            xt[:, jj, u, :], x_words[:, first : first + P], sel_of[g][:, j, :]
+                            xt_of[g, b][:, jj, u, :],
+                            x_words[:, first : first + P],
+                            sel_of[g][:, j, :],
                         )
-                nc.scalar.copy(
-                    out=grouped_words[:, b * bank_words : (b + 1) * bank_words].rearrange(
-                        "p (j n u) -> p j n u", j=BANK_EDGES, u=HALVES
-                    ),
-                    in_=xt[:].rearrange("p j u n -> p j n u"),
-                )
+
+        def empty_bank(copy, g, b):
+            grouped_words = grouped_of[g][:].bitcast(F32)
+            copy(
+                out=grouped_words[:, b * BANK_WORDS : (b + 1) * BANK_WORDS].rearrange(
+                    "p (j n u) -> p j n u", j=BANK_EDGES, u=HALVES
+                ),
+                in_=xt_of[g, b][:].rearrange("p j u n -> p j n u"),
+            )
 
         def quantise_group(g):
             codes_of[g] = mx_pool.tile([P, GROUP * P], U32, name="codes", align_bytes=64)
@@ -187,11 +190,20 @@ def tile_declayerj_pb_t_kernel(tc, h2, h_V, mask_attend, W3_w, W3_b, out):
         )
 
         for r in range(N_RUNS + 1):
-            for g in groups_of_run(r):
+            run = groups_of_run(r)
+            for g in run:
                 transpose_group(g)
-            for g in groups_of_run(r + 1):
-                build_selectors(g)
-            for g in groups_of_run(r):
+                grouped_of[g] = grouped_pool.tile(
+                    [P, GROUP * P * PACK], BF16, name="grouped", align_bytes=64
+                )
+                for b in range(GROUP_BANKS):
+                    if (g, b) != (run[-1], GROUP_BANKS - 1):
+                        empty_bank(nc.scalar.copy, g, b)
+            for g in run:
+                if g == run[len(run) // 2]:
+                    empty_bank(nc.vector.tensor_copy, run[-1], GROUP_BANKS - 1)
+                if g + GROUPS_PER_RUN < N_GROUPS:
+                    build_selectors(g + GROUPS_PER_RUN)
                 quantise_group(g)
             first = max(r * GROUPS_PER_RUN - LAG, 0)
             for g in range(first, min((r + 1) * GROUPS_PER_RUN - LAG, N_GROUPS)):

from contextlib import ExitStack

import concourse.masks as masks
import concourse.mybir as mybir

F32 = mybir.dt.float32
BF16 = mybir.dt.bfloat16
U32 = mybir.dt.uint32
U8 = mybir.dt.uint8
FP8X4 = mybir.dt.float8_e4m3fn_x4
MULT = mybir.AluOpType.mult
ADD = mybir.AluOpType.add

P = 128
PACK = 4
NODES = 2 * 256
EDGES = 32
M = 512
H = 256
SCALE = 30.0

NODE_TILES = NODES // P
WORDS = M // 2
HALVES = WORDS // P
GROUP = 4
GROUPS_PER_TILE = EDGES // GROUP
N_GROUPS = NODE_TILES * GROUPS_PER_TILE
BANK_EDGES = 2
GROUP_BANKS = GROUP // BANK_EDGES
BANK_WORDS = BANK_EDGES * WORDS
GROUPS_PER_RUN = 4
N_RUNS = N_GROUPS // GROUPS_PER_RUN
LAG = 2

FLOPS = 2 * NODES * EDGES * M * H


def tile_declayerj_pb_t_kernel(tc, h2, h_V, mask_attend, W3_w, W3_b, out):
    nc = tc.nc
    h2_nodes = h2.rearrange("b n k m -> (b n) (k m)").rearrange("(p i) f -> p i f", p=P)
    mask_nodes = mask_attend.rearrange("b n k -> (b n) k").rearrange("(p i) k -> p i k", p=P)
    hv_nodes = h_V.rearrange("b n h -> (b n) h").rearrange("(p i) h -> p i h", p=P)
    out_nodes = out.rearrange("b n h -> (b n) h").rearrange("(p i) h -> p i h", p=P)

    with ExitStack() as ctx:
        const = ctx.enter_context(tc.tile_pool(name="const", bufs=1))
        x_pool = ctx.enter_context(tc.tile_pool(name="x", bufs=N_GROUPS))
        sel_pool = ctx.enter_context(tc.tile_pool(name="sel", bufs=2 * GROUPS_PER_RUN))
        grouped_pool = ctx.enter_context(tc.tile_pool(name="grouped", bufs=GROUPS_PER_RUN + LAG))
        mx_pool = ctx.enter_context(tc.tile_pool(name="mx", bufs=2 * GROUPS_PER_RUN))
        tail = ctx.enter_context(tc.tile_pool(name="tail", bufs=2))
        xt_pool = ctx.enter_context(tc.psum_pool(name="xt", bufs=6))
        acc_pool = ctx.enter_context(tc.psum_pool(name="acc", bufs=2))
        ctx.enter_context(tc.manual_schedule())

        ident = const.tile([P, P], F32)
        masks.make_identity(nc, ident[:])
        ones = const.tile([P, P], BF16)
        nc.vector.memset(ones[:], 1.0)
        bias_rows = const.tile([P, H], BF16)
        nc.vector.memset(bias_rows[:], 0.0)

        mask_bf = const.tile([P, NODE_TILES, EDGES], BF16)
        nc.sync.dma_start(out=mask_bf[:], in_=mask_nodes)
        nc.sync.dma_start(out=bias_rows[0:1, :], in_=W3_b.unsqueeze(0))
        w_raw = const.tile([P, PACK, H], BF16)
        hv = const.tile([P, NODE_TILES, H], BF16)
        x_of = {}
        for g in range(N_GROUPS):
            i, q = divmod(g, GROUPS_PER_TILE)
            x_of[g] = x_pool.tile([P, GROUP * M], BF16, name="x")
            nc.sync.dma_start(
                out=x_of[g][:],
                in_=h2_nodes[:, i, q * GROUP * M : (q + 1) * GROUP * M],
            )
            if g == 0:
                nc.sync.dma_start(
                    out=w_raw[:].rearrange("p (u e) h -> p u (e h)", u=HALVES),
                    in_=W3_w.rearrange("(u p e) h -> p u (e h)", u=HALVES, p=P),
                )
            if g == GROUPS_PER_TILE - 1:
                nc.sync.dma_start(out=hv[:], in_=hv_nodes)

        bias_ps = acc_pool.tile([P, H], F32, name="bias_ps", tag="acc")
        nc.tensor.matmul(out=bias_ps[:], lhsT=ones[:], rhs=bias_rows[:], start=True, stop=True)
        bias_all = const.tile([P, H], F32)
        nc.scalar.copy(out=bias_all[:], in_=bias_ps[:])

        mask_f32 = const.tile([P, NODE_TILES, EDGES], F32)
        nc.vector.tensor_copy(out=mask_f32[:], in_=mask_bf[:])
        count = const.tile([P, NODE_TILES], F32)
        nc.vector.reduce_sum(out=count[:], in_=mask_f32[:], axis=mybir.AxisListType.X)
        count_scaled = const.tile([P, NODE_TILES], F32)
        nc.vector.tensor_scalar_mul(out=count_scaled[:], in0=count[:], scalar1=1.0 / SCALE)

        sel_of = {}
        xt_of = {}
        grouped_of = {}
        codes_of = {}
        scales_of = {}
        acc_of = {}

        def build_selectors(g):
            i, q = divmod(g, GROUPS_PER_TILE)
            sel_of[g] = sel_pool.tile([P, GROUP, P], F32, name="sel")
            for j in range(GROUP):
                k = q * GROUP + j
                nc.vector.tensor_scalar_mul(
                    out=sel_of[g][:, j, :], in0=ident[:], scalar1=mask_f32[:, i, k : k + 1]
                )

        def transpose_group(g):
            x_words = x_of[g][:].bitcast(F32)
            for b in range(GROUP_BANKS):
                xt_of[g, b] = xt_pool.tile([P, BANK_EDGES, HALVES, P], F32, name="xt")
                for jj in range(BANK_EDGES):
                    j = b * BANK_EDGES + jj
                    for u in range(HALVES):
                        first = j * WORDS + u * P
                        nc.tensor.transpose(
                            xt_of[g, b][:, jj, u, :],
                            x_words[:, first : first + P],
                            sel_of[g][:, j, :],
                        )

        def empty_bank(copy, g, b):
            grouped_words = grouped_of[g][:].bitcast(F32)
            copy(
                out=grouped_words[:, b * BANK_WORDS : (b + 1) * BANK_WORDS].rearrange(
                    "p (j n u) -> p j n u", j=BANK_EDGES, u=HALVES
                ),
                in_=xt_of[g, b][:].rearrange("p j u n -> p j n u"),
            )

        def quantise_group(g):
            codes_of[g] = mx_pool.tile([P, GROUP * P], U32, name="codes", align_bytes=64)
            scales_of[g] = mx_pool.tile([P, GROUP * P], U8, name="scales", align_bytes=64)
            nc.vector.quantize_mx(
                out=codes_of[g][:].bitcast(FP8X4), scales=scales_of[g][:], in_=grouped_of[g][:]
            )

        def multiply_group(g):
            i, q = divmod(g, GROUPS_PER_TILE)
            if q == 0:
                acc_of[i] = acc_pool.tile([P, H], F32, name="acc", tag="acc")
            for j in range(GROUP):
                k = q * GROUP + j
                nodes = slice(j * P, (j + 1) * P)
                nc.tensor.matmul_mx(
                    out=acc_of[i][:],
                    lhsT=codes_of[g][:, nodes].bitcast(FP8X4),
                    lhsT_scale=scales_of[g][:, nodes],
                    rhs=w_codes[:].bitcast(FP8X4),
                    rhs_scale=w_scales[:],
                    start=(k == 0),
                    stop=(k == EDGES - 1),
                )
            if q == GROUPS_PER_TILE - 1:
                finish_node_tile(i)

        def finish_node_tile(i):
            rest = tail.tile([P, H], F32, name="rest")
            nc.vector.scalar_tensor_tensor(
                out=rest[:],
                in0=bias_all[:],
                scalar=count_scaled[:, i : i + 1],
                in1=hv[:, i, :],
                op0=MULT,
                op1=ADD,
            )
            result = tail.tile([P, H], F32, name="result")
            nc.vector.scalar_tensor_tensor(
                out=result[:], in0=acc_of[i][:], scalar=1.0 / SCALE, in1=rest[:], op0=MULT, op1=ADD
            )
            nc.sync.dma_start(out=out_nodes[:, i, :], in_=result[:])

        def groups_of_run(r):
            return range(r * GROUPS_PER_RUN, min((r + 1) * GROUPS_PER_RUN, N_GROUPS))

        for g in groups_of_run(0):
            build_selectors(g)
        w_grouped = const.tile([P, H, PACK], BF16, align_bytes=64)
        nc.vector.tensor_copy(out=w_grouped[:], in_=w_raw[:].rearrange("p t h -> p h t"))
        w_codes = const.tile([P, H], U32, align_bytes=64)
        w_scales = const.tile([P, H], U8, align_bytes=64)
        nc.vector.quantize_mx(
            out=w_codes[:].bitcast(FP8X4),
            scales=w_scales[:],
            in_=w_grouped[:].rearrange("p h t -> p (h t)"),
        )

        for r in range(N_RUNS + 1):
            run = groups_of_run(r)
            for g in run:
                transpose_group(g)
                grouped_of[g] = grouped_pool.tile(
                    [P, GROUP * P * PACK], BF16, name="grouped", align_bytes=64
                )
                for b in range(GROUP_BANKS):
                    if (g, b) != (run[-1], GROUP_BANKS - 1):
                        empty_bank(nc.scalar.copy, g, b)
            for g in run:
                if g == run[len(run) // 2]:
                    empty_bank(nc.vector.tensor_copy, run[-1], GROUP_BANKS - 1)
                if g + GROUPS_PER_RUN < N_GROUPS:
                    build_selectors(g + GROUPS_PER_RUN)
                quantise_group(g)
            first = max(r * GROUPS_PER_RUN - LAG, 0)
            for g in range(first, min((r + 1) * GROUPS_PER_RUN - LAG, N_GROUPS)):
                multiply_group(g)
